import numpy as np
import ml_dtypes


def mxq(x, axis, fmt="e4m3"):
    dtype, down = {"e4m3": (ml_dtypes.float8_e4m3fn, 7), "e5m2": (ml_dtypes.float8_e5m2, 14)}[fmt]
    v = np.moveaxis(np.asarray(x, np.float32).astype(ml_dtypes.bfloat16).astype(np.float64), axis, -1)
    blocks = v.reshape(v.shape[:-1] + (-1, 32))
    amax = np.abs(blocks).max(-1, keepdims=True)
    byte = np.maximum(np.where(amax > 0, np.frexp(amax)[1] - 1 + 127, 0) - down, 1)
    scale = np.exp2(byte - 127.0)
    codes = (blocks / scale).astype(np.float32).astype(dtype).astype(np.float64)
    return np.moveaxis((codes * scale).reshape(v.shape), -1, axis)


WIDE = False


def mx_kscale(k):
    if not WIDE:
        return np.ones(k)
    levels = np.array([10, -10, 5, -5, 0])
    a = np.random.permutation(np.resize(levels, k // 512 * 4)).reshape(k // 512, 4)
    idx = np.arange(k)
    return np.exp2(a[idx // 512, idx % 128 // 32])


BF16 = ml_dtypes.bfloat16


def bf(x):
    return np.asarray(x, np.float32).astype(BF16)


def f64(x):
    return np.asarray(x).astype(np.float64)


E2M1 = np.array([0.0, 0.5, 1.0, 1.5, 2.0, 3.0, 4.0, 6.0, -0.0, -0.5, -1.0, -1.5, -2.0, -3.0, -4.0, -6.0])


def pack_weight(w, fmt):
    k, n = w.shape
    w = f64(bf(w)).reshape(k // 32, 32, n)
    amax = np.abs(w).max(1)
    if fmt == "e4m3":
        byte = np.frexp(amax)[1] - 1 + 127 - 7
    else:
        mant, ex = np.frexp(amax / 6.0)
        byte = np.where(mant > 0.5, ex, ex - 1) + 127
    byte = np.clip(np.where(amax > 0, byte, 1), 1, 254)
    scaled = (w * np.exp2(127.0 - byte)[:, None, :]).reshape(k, n).astype(np.float32)
    by_word = np.ascontiguousarray(scaled.reshape(k // 512, 128, 4, n).transpose(0, 1, 3, 2))
    if fmt == "e4m3":
        words = by_word.astype(ml_dtypes.float8_e4m3fn).view(np.uint8)
    else:
        c = by_word.astype(ml_dtypes.float4_e2m1fn).view(np.uint8) & 0xF
        words = c[..., 0::2] | (c[..., 1::2] << 4)
    return np.ascontiguousarray(words), np.ascontiguousarray(byte.astype(np.uint8).reshape(k // 512, 16, n))


def unpack_weight(words, scales, fmt):
    g, p, n, _ = words.shape
    if fmt == "e4m3":
        vals = np.ascontiguousarray(words).view(ml_dtypes.float8_e4m3fn).astype(np.float64)
    else:
        nib = np.empty((g, p, n, 4), np.uint8)
        nib[..., 0::2] = words & 0xF
        nib[..., 1::2] = words >> 4
        vals = E2M1[nib]
    vals = vals * np.repeat(np.exp2(scales.astype(np.float64) - 127.0), 8, axis=1)[..., None]
    return vals.transpose(0, 1, 3, 2).reshape(g * 512, n)


B, IN_F, OUT_F, N_ACT = 2048, 1024, 1024, 4
FMT = "e4m3"


def sigmoid(v):
    return 1.0 / (1.0 + np.exp(-v))


def setup_inputs():
    s = mx_kscale(IN_F)
    limit = np.sqrt(6.0 / (IN_F + OUT_F))
    x = bf(np.random.standard_normal((B, IN_F)) * s)
    w = np.random.uniform(-limit, limit, (OUT_F, IN_F)) / s[None, :]
    words, scales = pack_weight(np.ascontiguousarray(w.T), FMT)
    b = bf(np.random.standard_normal(OUT_F) * 0.1)
    return {"input": x,
            "W_words": words,
            "W_scales": scales,
            "b": b}


def _apply_cyclic_acts(y):
    Bb, O = y.shape
    yg = y.reshape(Bb, O // N_ACT, N_ACT)
    out = np.stack([
        np.tanh(yg[..., 0]),
        np.sin(yg[..., 1]),
        np.maximum(yg[..., 2], 0.0),
        sigmoid(yg[..., 3]),
    ], axis=-1)
    return out.reshape(Bb, O)


def reference(input, W_words, W_scales, b):
    y = (mxq(f64(input), 1, "e4m3") @ unpack_weight(W_words, W_scales, FMT)) + f64(b)
    return _apply_cyclic_acts(y)

@@ -1,0 +1,206 @@
+import math
+from contextlib import ExitStack
+
+import concourse.mybir as mybir
+from concourse.masks import make_identity
+
+F32 = mybir.dt.float32
+BF16 = mybir.dt.bfloat16
+I32 = mybir.dt.int32
+U8 = mybir.dt.uint8
+U32 = mybir.dt.uint32
+FP8X4 = mybir.dt.float8_e4m3fn_x4
+ACT = mybir.ActivationFunctionType
+ALU = mybir.AluOpType
+
+ROWS, IN_F, OUT_F = 2048, 1024, 1024
+FLOPS = 2 * ROWS * IN_F * OUT_F
+
+P = 128
+K_PASS = 4 * P
+PASSES = IN_F // K_PASS
+N_BANK = 512
+BANKS = OUT_F // N_BANK
+KINDS = 4
+PER_KIND = OUT_F // KINDS
+PER_KIND_BANK = N_BANK // KINDS
+ROW_TILES = ROWS // P
+TILES = 2
+BLOCKS = ROW_TILES // TILES
+
+TWO_PI = 2.0 * math.pi
+ROUND_MAGIC = 1.5 * 2.0**23
+
+
+def tile_vdl_kernel(tc, x, w_words, w_scales, b, out):
+    nc = tc.nc
+    x_rows = x.rearrange("(p i) k -> p i k", i=ROW_TILES)
+    out_rows = out.rearrange("(p i) n -> p i n", i=ROW_TILES)
+
+    with ExitStack() as ctx:
+        consts = ctx.enter_context(tc.tile_pool(name="consts", bufs=1))
+        x_pool = ctx.enter_context(tc.tile_pool(name="x", bufs=BLOCKS))
+        quant_pool = ctx.enter_context(tc.tile_pool(name="quant", bufs=3))
+        kinds_pool = ctx.enter_context(tc.tile_pool(name="kinds", bufs=4))
+        out_pool = ctx.enter_context(tc.tile_pool(name="outs", bufs=3))
+        psum_t = ctx.enter_context(tc.psum_pool(name="psum_t", bufs=2))
+        psum_y = ctx.enter_context(tc.psum_pool(name="psum_y", bufs=6))
+
+        w_planes = consts.tile([P, PASSES, OUT_F], U8, align_bytes=64)
+        nc.vector.memset(w_planes[:].bitcast(I32), 0)
+        x_blocks = []
+        for blk in range(BLOCKS):
+            x_blk = x_pool.tile([P, TILES, IN_F], BF16)
+            x_blocks.append(x_blk)
+        nc.sync.dma_start(out=x_blocks[0][:], in_=x_rows[:, 0:TILES, :])
+        scale_rows = w_scales.rearrange("g (Q r) n -> r Q g n", r=4)
+        for r in range(4):
+            nc.sync.dma_start(out=w_planes[r:P:32, :, :].bitcast(I32), in_=scale_rows[r].bitcast(I32))
+        w_codes = consts.tile([P, PASSES, 4 * OUT_F], U8, align_bytes=64)
+        for g in range(PASSES):
+            nc.sync.dma_start(
+                out=w_codes[:, g, :].bitcast(I32),
+                in_=w_words[g].rearrange("p n t -> p (n t)").bitcast(I32),
+            )
+        for blk in range(1, BLOCKS):
+            nc.sync.dma_start(out=x_blocks[blk][:], in_=x_rows[:, blk * TILES : (blk + 1) * TILES, :])
+
+        warm = consts.tile([P, 1], F32)
+        nc.vector.memset(warm[:], 0.0)
+        nc.scalar.activation(out=warm[:], in_=warm[:], func=ACT.Silu)
+
+        ident = consts.tile([P, P], F32)
+        make_identity(nc, ident[:])
+
+        ones = consts.tile([P, P], BF16)
+        nc.vector.memset(ones[:], 1.0)
+        b_rows = consts.tile([P, OUT_F], BF16)
+        nc.vector.memset(b_rows[:], 0.0)
+        nc.scalar.dma_start(out=b_rows[0:1, :], in_=b.rearrange("(o n) -> o n", o=1))
+        bias_turns = consts.tile([P, KINDS, PER_KIND], F32)
+        for h in range(BANKS):
+            b_all = psum_y.tile([P, N_BANK], F32, name="acc")
+            nc.tensor.matmul(
+                out=b_all[:], lhsT=ones[:], rhs=b_rows[:, h * N_BANK : (h + 1) * N_BANK], start=True, stop=True
+            )
+            nc.vector.tensor_scalar(
+                out=bias_turns[:, :, h * PER_KIND_BANK : (h + 1) * PER_KIND_BANK],
+                in0=b_all[:].rearrange("p (j a) -> p a j", a=KINDS),
+                scalar1=1.0 / TWO_PI,
+                scalar2=None,
+                op0=ALU.mult,
+            )
+
+        grouped_of = {}
+        codes_of = {}
+        acc_of = {}
+        kinds_of = {}
+
+        def transpose_block(blk):
+            grouped = quant_pool.tile([P, TILES, IN_F], BF16, align_bytes=64)
+            for t in range(TILES):
+                words = x_blocks[blk][:, t, :].bitcast(F32)
+                flipped = psum_t.tile([P, PASSES, 2, P], F32)
+                for g in range(PASSES):
+                    for u in range(2):
+                        nc.tensor.transpose(
+                            flipped[:, g, u, :], words[:, 256 * g + u : 256 * (g + 1) : 2], ident[:]
+                        )
+                nc.scalar.copy(
+                    out=grouped[:, t, :].bitcast(F32).rearrange("p (g m u) -> p g m u", g=PASSES, u=2),
+                    in_=flipped[:].rearrange("p g u m -> p g m u"),
+                )
+            grouped_of[blk] = grouped
+
+        def quantise_block(blk):
+            x_codes = quant_pool.tile([P, TILES, PASSES, P], U32, align_bytes=64)
+            x_scales = quant_pool.tile([P, TILES, PASSES, P], U8, align_bytes=64)
+            nc.vector.quantize_mx(
+                out=x_codes[:].rearrange("p t g m -> p (t g m)").bitcast(FP8X4),
+                scales=x_scales[:].rearrange("p t g m -> p (t g m)"),
+                in_=grouped_of.pop(blk)[:].rearrange("p t c -> p (t c)"),
+            )
+            codes_of[blk] = (x_codes, x_scales)
+
+        def multiply_block(blk):
+            x_codes, x_scales = codes_of.pop(blk)
+            accs = []
+            for t in range(TILES):
+                for h in range(BANKS):
+                    acc = psum_y.tile([P, N_BANK], F32)
+                    for g in range(PASSES):
+                        nc.tensor.matmul_mx(
+                            out=acc[:],
+                            lhsT=x_codes[:, t, g, :].bitcast(FP8X4),
+                            lhsT_scale=x_scales[:, t, g, :],
+                            rhs=w_codes[:, g, 4 * h * N_BANK : 4 * (h + 1) * N_BANK].bitcast(FP8X4),
+                            rhs_scale=w_planes[:, g, h * N_BANK : (h + 1) * N_BANK],
+                            start=(g == 0),
+                            stop=(g == PASSES - 1),
+                        )
+                    accs.append(acc)
+            acc_of[blk] = accs
+
+        def add_bias_block(blk):
+            accs = acc_of.pop(blk)
+            kinds = kinds_pool.tile([P, KINDS, TILES, PER_KIND], F32)
+            for t in range(TILES):
+                for h in range(BANKS):
+                    cols = slice(h * PER_KIND_BANK, (h + 1) * PER_KIND_BANK)
+                    nc.vector.scalar_tensor_tensor(
+                        out=kinds[:, :, t, cols],
+                        in0=accs[t * BANKS + h][:].rearrange("p (j a) -> p a j", a=KINDS),
+                        scalar=1.0 / TWO_PI,
+                        in1=bias_turns[:, :, cols],
+                        op0=ALU.mult,
+                        op1=ALU.add,
+                    )
+            shifted = kinds_pool.tile([P, TILES, PER_KIND], F32)
+            wrapped = kinds_pool.tile([P, TILES, PER_KIND], F32)
+            nc.vector.tensor_scalar(
+                out=shifted[:], in0=kinds[:, 1], scalar1=ROUND_MAGIC, scalar2=None, op0=ALU.add
+            )
+            nc.vector.scalar_tensor_tensor(
+                out=wrapped[:],
+                in0=shifted[:],
+                scalar=ROUND_MAGIC,
+                in1=kinds[:, 1],
+                op0=ALU.subtract,
+                op1=ALU.subtract,
+            )
+            kinds_of[blk] = (kinds, wrapped)
+
+        def activate_block(blk):
+            kinds, wrapped = kinds_of[blk]
+            nc.scalar.activation(out=kinds[:, 3], in_=kinds[:, 3], func=ACT.Tanh, scale=TWO_PI / 2.0)
+            nc.scalar.activation(out=kinds[:, 0], in_=kinds[:, 0], func=ACT.Tanh, scale=TWO_PI)
+            nc.scalar.activation(out=kinds[:, 2], in_=kinds[:, 2], func=ACT.Relu, scale=TWO_PI)
+            nc.scalar.activation(out=kinds[:, 1], in_=wrapped[:], func=ACT.Sin, scale=-TWO_PI)
+
+        def finish_block(blk):
+            kinds, wrapped = kinds_of.pop(blk)
+            nc.vector.tensor_scalar(
+                out=kinds[:, 3], in0=kinds[:, 3], scalar1=0.5, scalar2=0.5, op0=ALU.mult, op1=ALU.add
+            )
+            result = out_pool.tile([P, TILES, OUT_F], F32)
+            nc.scalar.copy(
+                out=result[:, 0, :].rearrange("p (j a) -> p j a", a=KINDS),
+                in_=kinds[:, :, 0, :].rearrange("p a j -> p j a"),
+            )
+            nc.vector.tensor_copy(
+                out=result[:, 1, :].rearrange("p (j a) -> p j a", a=KINDS),
+                in_=kinds[:, :, 1, :].rearrange("p a j -> p j a"),
+            )
+            nc.sync.dma_start(out=out_rows[:, blk * TILES : (blk + 1) * TILES, :], in_=result[:])
+
+        for step in range(BLOCKS + 3):
+            if step < BLOCKS:
+                transpose_block(step)
+            if 0 <= step - 1 < BLOCKS:
+                quantise_block(step - 1)
+                multiply_block(step - 1)
+            if 0 <= step - 2 < BLOCKS:
+                add_bias_block(step - 2)
+                activate_block(step - 2)
+            if 0 <= step - 3 < BLOCKS:
+                finish_block(step - 3)

@@ -28,6 +28,8 @@ ROW_TILES = ROWS // P
 TILES = 2
 BLOCKS = ROW_TILES // TILES
 
+SCALAR_GROUPS = 192
+
 TWO_PI = 2.0 * math.pi
 ROUND_MAGIC = 1.5 * 2.0**23
 
@@ -39,7 +41,7 @@ def tile_vdl_kernel(tc, x, w_words, w_scales, b, out):
 
     with ExitStack() as ctx:
         consts = ctx.enter_context(tc.tile_pool(name="consts", bufs=1))
-        x_pool = ctx.enter_context(tc.tile_pool(name="x", bufs=BLOCKS))
+        x_pool = ctx.enter_context(tc.tile_pool(name="x", bufs=ROW_TILES))
         quant_pool = ctx.enter_context(tc.tile_pool(name="quant", bufs=3))
         kinds_pool = ctx.enter_context(tc.tile_pool(name="kinds", bufs=4))
         out_pool = ctx.enter_context(tc.tile_pool(name="outs", bufs=3))
@@ -48,11 +50,15 @@ def tile_vdl_kernel(tc, x, w_words, w_scales, b, out):
 
         w_planes = consts.tile([P, PASSES, OUT_F], U8, align_bytes=64)
         nc.vector.memset(w_planes[:].bitcast(I32), 0)
-        x_blocks = []
-        for blk in range(BLOCKS):
-            x_blk = x_pool.tile([P, TILES, IN_F], BF16)
-            x_blocks.append(x_blk)
-        nc.sync.dma_start(out=x_blocks[0][:], in_=x_rows[:, 0:TILES, :])
+        b_rows = consts.tile([P, OUT_F], BF16)
+        nc.vector.memset(b_rows[:], 0.0)
+        nc.scalar.dma_start(out=b_rows[0:1, :], in_=b.rearrange("(o n) -> o n", o=1))
+        x_tiles = []
+        for i in range(ROW_TILES):
+            x_tile = x_pool.tile([P, IN_F], BF16)
+            x_tiles.append(x_tile)
+        for i in range(TILES):
+            nc.sync.dma_start(out=x_tiles[i][:], in_=x_rows[:, i, :])
         scale_rows = w_scales.rearrange("g (Q r) n -> r Q g n", r=4)
         for r in range(4):
             nc.sync.dma_start(out=w_planes[r:P:32, :, :].bitcast(I32), in_=scale_rows[r].bitcast(I32))
@@ -62,8 +68,8 @@ def tile_vdl_kernel(tc, x, w_words, w_scales, b, out):
                 out=w_codes[:, g, :].bitcast(I32),
                 in_=w_words[g].rearrange("p n t -> p (n t)").bitcast(I32),
             )
-        for blk in range(1, BLOCKS):
-            nc.sync.dma_start(out=x_blocks[blk][:], in_=x_rows[:, blk * TILES : (blk + 1) * TILES, :])
+        for i in range(TILES, ROW_TILES):
+            nc.sync.dma_start(out=x_tiles[i][:], in_=x_rows[:, i, :])
 
         warm = consts.tile([P, 1], F32)
         nc.vector.memset(warm[:], 0.0)
@@ -74,9 +80,6 @@ def tile_vdl_kernel(tc, x, w_words, w_scales, b, out):
 
         ones = consts.tile([P, P], BF16)
         nc.vector.memset(ones[:], 1.0)
-        b_rows = consts.tile([P, OUT_F], BF16)
-        nc.vector.memset(b_rows[:], 0.0)
-        nc.scalar.dma_start(out=b_rows[0:1, :], in_=b.rearrange("(o n) -> o n", o=1))
         bias_turns = consts.tile([P, KINDS, PER_KIND], F32)
         for h in range(BANKS):
             b_all = psum_y.tile([P, N_BANK], F32, name="acc")
@@ -99,7 +102,7 @@ def tile_vdl_kernel(tc, x, w_words, w_scales, b, out):
         def transpose_block(blk):
             grouped = quant_pool.tile([P, TILES, IN_F], BF16, align_bytes=64)
             for t in range(TILES):
-                words = x_blocks[blk][:, t, :].bitcast(F32)
+                words = x_tiles[blk * TILES + t][:].bitcast(F32)
                 flipped = psum_t.tile([P, PASSES, 2, P], F32)
                 for g in range(PASSES):
                     for u in range(2):
@@ -157,8 +160,8 @@ def tile_vdl_kernel(tc, x, w_words, w_scales, b, out):
                     )
             shifted = kinds_pool.tile([P, TILES, PER_KIND], F32)
             wrapped = kinds_pool.tile([P, TILES, PER_KIND], F32)
-            nc.vector.tensor_scalar(
-                out=shifted[:], in0=kinds[:, 1], scalar1=ROUND_MAGIC, scalar2=None, op0=ALU.add
+            nc.gpsimd.tensor_scalar(
+                out=shifted[:], in0=kinds[:, 1], scalar1=1.0, scalar2=ROUND_MAGIC, op0=ALU.mult, op1=ALU.add
             )
             nc.vector.scalar_tensor_tensor(
                 out=wrapped[:],
@@ -179,18 +182,14 @@ def tile_vdl_kernel(tc, x, w_words, w_scales, b, out):
 
         def finish_block(blk):
             kinds, wrapped = kinds_of.pop(blk)
-            nc.vector.tensor_scalar(
+            nc.gpsimd.tensor_scalar(
                 out=kinds[:, 3], in0=kinds[:, 3], scalar1=0.5, scalar2=0.5, op0=ALU.mult, op1=ALU.add
             )
             result = out_pool.tile([P, TILES, OUT_F], F32)
-            nc.scalar.copy(
-                out=result[:, 0, :].rearrange("p (j a) -> p j a", a=KINDS),
-                in_=kinds[:, :, 0, :].rearrange("p a j -> p j a"),
-            )
-            nc.vector.tensor_copy(
-                out=result[:, 1, :].rearrange("p (j a) -> p j a", a=KINDS),
-                in_=kinds[:, :, 1, :].rearrange("p a j -> p j a"),
-            )
+            in_order = result[:].rearrange("p t (j a) -> p (t j) a", a=KINDS)
+            by_kind = kinds[:].rearrange("p a t j -> p (t j) a")
+            nc.scalar.copy(out=in_order[:, 0:SCALAR_GROUPS, :], in_=by_kind[:, 0:SCALAR_GROUPS, :])
+            nc.vector.tensor_copy(out=in_order[:, SCALAR_GROUPS:, :], in_=by_kind[:, SCALAR_GROUPS:, :])
             nc.sync.dma_start(out=out_rows[:, blk * TILES : (blk + 1) * TILES, :], in_=result[:])
 
         for step in range(BLOCKS + 3):

@@ -25,10 +25,10 @@ KINDS = 4
 PER_KIND = OUT_F // KINDS
 PER_KIND_BANK = N_BANK // KINDS
 ROW_TILES = ROWS // P
-TILES = 2
+TILES = 1
 BLOCKS = ROW_TILES // TILES
 
-SCALAR_GROUPS = 192
+SCALAR_GROUPS = 144
 
 TWO_PI = 2.0 * math.pi
 ROUND_MAGIC = 1.5 * 2.0**23
@@ -42,9 +42,9 @@ def tile_vdl_kernel(tc, x, w_words, w_scales, b, out):
     with ExitStack() as ctx:
         consts = ctx.enter_context(tc.tile_pool(name="consts", bufs=1))
         x_pool = ctx.enter_context(tc.tile_pool(name="x", bufs=ROW_TILES))
-        quant_pool = ctx.enter_context(tc.tile_pool(name="quant", bufs=3))
-        kinds_pool = ctx.enter_context(tc.tile_pool(name="kinds", bufs=4))
-        out_pool = ctx.enter_context(tc.tile_pool(name="outs", bufs=3))
+        quant_pool = ctx.enter_context(tc.tile_pool(name="quant", bufs=4))
+        kinds_pool = ctx.enter_context(tc.tile_pool(name="kinds", bufs=6))
+        out_pool = ctx.enter_context(tc.tile_pool(name="outs", bufs=4))
         psum_t = ctx.enter_context(tc.psum_pool(name="psum_t", bufs=2))
         psum_y = ctx.enter_context(tc.psum_pool(name="psum_y", bufs=6))
 
@@ -160,8 +160,8 @@ def tile_vdl_kernel(tc, x, w_words, w_scales, b, out):
                     )
             shifted = kinds_pool.tile([P, TILES, PER_KIND], F32)
             wrapped = kinds_pool.tile([P, TILES, PER_KIND], F32)
-            nc.gpsimd.tensor_scalar(
-                out=shifted[:], in0=kinds[:, 1], scalar1=1.0, scalar2=ROUND_MAGIC, op0=ALU.mult, op1=ALU.add
+            nc.vector.tensor_scalar(
+                out=shifted[:], in0=kinds[:, 1], scalar1=ROUND_MAGIC, scalar2=None, op0=ALU.add
             )
             nc.vector.scalar_tensor_tensor(
                 out=wrapped[:],
@@ -182,7 +182,7 @@ def tile_vdl_kernel(tc, x, w_words, w_scales, b, out):
 
         def finish_block(blk):
             kinds, wrapped = kinds_of.pop(blk)
-            nc.gpsimd.tensor_scalar(
+            nc.vector.tensor_scalar(
                 out=kinds[:, 3], in0=kinds[:, 3], scalar1=0.5, scalar2=0.5, op0=ALU.mult, op1=ALU.add
             )
             result = out_pool.tile([P, TILES, OUT_F], F32)

@@ -25,10 +25,11 @@ KINDS = 4
 PER_KIND = OUT_F // KINDS
 PER_KIND_BANK = N_BANK // KINDS
 ROW_TILES = ROWS // P
-TILES = 1
+TILES = 2
 BLOCKS = ROW_TILES // TILES
 
-SCALAR_GROUPS = 144
+SCALAR_GROUPS = 192
+GPSIMD_GROUPS = 256
 
 TWO_PI = 2.0 * math.pi
 ROUND_MAGIC = 1.5 * 2.0**23
@@ -42,9 +43,9 @@ def tile_vdl_kernel(tc, x, w_words, w_scales, b, out):
     with ExitStack() as ctx:
         consts = ctx.enter_context(tc.tile_pool(name="consts", bufs=1))
         x_pool = ctx.enter_context(tc.tile_pool(name="x", bufs=ROW_TILES))
-        quant_pool = ctx.enter_context(tc.tile_pool(name="quant", bufs=4))
-        kinds_pool = ctx.enter_context(tc.tile_pool(name="kinds", bufs=6))
-        out_pool = ctx.enter_context(tc.tile_pool(name="outs", bufs=4))
+        quant_pool = ctx.enter_context(tc.tile_pool(name="quant", bufs=3))
+        kinds_pool = ctx.enter_context(tc.tile_pool(name="kinds", bufs=4))
+        out_pool = ctx.enter_context(tc.tile_pool(name="outs", bufs=3))
         psum_t = ctx.enter_context(tc.psum_pool(name="psum_t", bufs=2))
         psum_y = ctx.enter_context(tc.psum_pool(name="psum_y", bufs=6))
 
@@ -188,8 +189,18 @@ def tile_vdl_kernel(tc, x, w_words, w_scales, b, out):
             result = out_pool.tile([P, TILES, OUT_F], F32)
             in_order = result[:].rearrange("p t (j a) -> p (t j) a", a=KINDS)
             by_kind = kinds[:].rearrange("p a t j -> p (t j) a")
-            nc.scalar.copy(out=in_order[:, 0:SCALAR_GROUPS, :], in_=by_kind[:, 0:SCALAR_GROUPS, :])
-            nc.vector.tensor_copy(out=in_order[:, SCALAR_GROUPS:, :], in_=by_kind[:, SCALAR_GROUPS:, :])
+            cut_1 = SCALAR_GROUPS
+            cut_2 = SCALAR_GROUPS + GPSIMD_GROUPS
+            nc.scalar.copy(out=in_order[:, 0:cut_1, :], in_=by_kind[:, 0:cut_1, :])
+            nc.gpsimd.tensor_scalar(
+                out=in_order[:, cut_1:cut_2, :],
+                in0=by_kind[:, cut_1:cut_2, :],
+                scalar1=1.0,
+                scalar2=0.0,
+                op0=ALU.mult,
+                op1=ALU.add,
+            )
+            nc.vector.tensor_copy(out=in_order[:, cut_2:, :], in_=by_kind[:, cut_2:, :])
             nc.sync.dma_start(out=out_rows[:, blk * TILES : (blk + 1) * TILES, :], in_=result[:])
 
         for step in range(BLOCKS + 3):

@@ -22,14 +22,12 @@ PASSES = IN_F // K_PASS
 N_BANK = 512
 BANKS = OUT_F // N_BANK
 KINDS = 4
+TANH, SIN, RELU, SIGMOID = 0, 1, 2, 3
 PER_KIND = OUT_F // KINDS
 PER_KIND_BANK = N_BANK // KINDS
 ROW_TILES = ROWS // P
 TILES = 2
 BLOCKS = ROW_TILES // TILES
-
-SCALAR_GROUPS = 192
-GPSIMD_GROUPS = 256
 
 TWO_PI = 2.0 * math.pi
 ROUND_MAGIC = 1.5 * 2.0**23
@@ -43,11 +41,13 @@ def tile_vdl_kernel(tc, x, w_words, w_scales, b, out):
     with ExitStack() as ctx:
         consts = ctx.enter_context(tc.tile_pool(name="consts", bufs=1))
         x_pool = ctx.enter_context(tc.tile_pool(name="x", bufs=ROW_TILES))
-        quant_pool = ctx.enter_context(tc.tile_pool(name="quant", bufs=3))
-        kinds_pool = ctx.enter_context(tc.tile_pool(name="kinds", bufs=4))
+        grouped_pool = ctx.enter_context(tc.tile_pool(name="grouped", bufs=2 * TILES))
+        codes_pool = ctx.enter_context(tc.tile_pool(name="codes", bufs=3 * TILES))
+        kinds_pool = ctx.enter_context(tc.tile_pool(name="kinds", bufs=3))
         out_pool = ctx.enter_context(tc.tile_pool(name="outs", bufs=3))
-        psum_t = ctx.enter_context(tc.psum_pool(name="psum_t", bufs=2))
+        psum_t = ctx.enter_context(tc.psum_pool(name="psum_t", bufs=TILES))
         psum_y = ctx.enter_context(tc.psum_pool(name="psum_y", bufs=6))
+        ctx.enter_context(tc.manual_schedule())
 
         w_planes = consts.tile([P, PASSES, OUT_F], U8, align_bytes=64)
         nc.vector.memset(w_planes[:].bitcast(I32), 0)
@@ -58,7 +58,7 @@ def tile_vdl_kernel(tc, x, w_words, w_scales, b, out):
         for i in range(ROW_TILES):
             x_tile = x_pool.tile([P, IN_F], BF16)
             x_tiles.append(x_tile)
-        for i in range(TILES):
+        for i in range(2 * TILES):
             nc.sync.dma_start(out=x_tiles[i][:], in_=x_rows[:, i, :])
         scale_rows = w_scales.rearrange("g (Q r) n -> r Q g n", r=4)
         for r in range(4):
@@ -69,7 +69,7 @@ def tile_vdl_kernel(tc, x, w_words, w_scales, b, out):
                 out=w_codes[:, g, :].bitcast(I32),
                 in_=w_words[g].rearrange("p n t -> p (n t)").bitcast(I32),
             )
-        for i in range(TILES, ROW_TILES):
+        for i in range(2 * TILES, ROW_TILES):
             nc.sync.dma_start(out=x_tiles[i][:], in_=x_rows[:, i, :])
 
         warm = consts.tile([P, 1], F32)
@@ -95,122 +95,157 @@ def tile_vdl_kernel(tc, x, w_words, w_scales, b, out):
                 op0=ALU.mult,
             )
 
+        flipped_of = {}
         grouped_of = {}
         codes_of = {}
         acc_of = {}
         kinds_of = {}
+        wrap_of = {}
+
+        def tiles_of(blk):
+            return range(blk * TILES, (blk + 1) * TILES)
 
         def transpose_block(blk):
-            grouped = quant_pool.tile([P, TILES, IN_F], BF16, align_bytes=64)
-            for t in range(TILES):
-                words = x_tiles[blk * TILES + t][:].bitcast(F32)
+            for i in tiles_of(blk):
+                words = x_tiles[i][:].bitcast(F32)
                 flipped = psum_t.tile([P, PASSES, 2, P], F32)
                 for g in range(PASSES):
                     for u in range(2):
                         nc.tensor.transpose(
                             flipped[:, g, u, :], words[:, 256 * g + u : 256 * (g + 1) : 2], ident[:]
                         )
-                nc.scalar.copy(
-                    out=grouped[:, t, :].bitcast(F32).rearrange("p (g m u) -> p g m u", g=PASSES, u=2),
-                    in_=flipped[:].rearrange("p g u m -> p g m u"),
-                )
-            grouped_of[blk] = grouped
+                flipped_of[i] = flipped
 
-        def quantise_block(blk):
-            x_codes = quant_pool.tile([P, TILES, PASSES, P], U32, align_bytes=64)
-            x_scales = quant_pool.tile([P, TILES, PASSES, P], U8, align_bytes=64)
+        def regroup_block(blk):
+            for i in tiles_of(blk):
+                grouped = grouped_pool.tile([P, IN_F], BF16, align_bytes=64)
+                nc.scalar.copy(
+                    out=grouped[:].bitcast(F32).rearrange("p (g m u) -> p g m u", g=PASSES, u=2),
+                    in_=flipped_of.pop(i)[:].rearrange("p g u m -> p g m u"),
+                )
+                grouped_of[i] = grouped
+
+        def quantise_tile(i):
+            x_codes = codes_pool.tile([P, PASSES, P], U32, align_bytes=64)
+            x_scales = codes_pool.tile([P, PASSES, P], U8, align_bytes=64)
             nc.vector.quantize_mx(
-                out=x_codes[:].rearrange("p t g m -> p (t g m)").bitcast(FP8X4),
-                scales=x_scales[:].rearrange("p t g m -> p (t g m)"),
-                in_=grouped_of.pop(blk)[:].rearrange("p t c -> p (t c)"),
+                out=x_codes[:].rearrange("p g m -> p (g m)").bitcast(FP8X4),
+                scales=x_scales[:].rearrange("p g m -> p (g m)"),
+                in_=grouped_of.pop(i)[:],
             )
-            codes_of[blk] = (x_codes, x_scales)
+            codes_of[i] = (x_codes, x_scales)
 
         def multiply_block(blk):
-            x_codes, x_scales = codes_of.pop(blk)
-            accs = []
-            for t in range(TILES):
+            for i in tiles_of(blk):
+                x_codes, x_scales = codes_of.pop(i)
                 for h in range(BANKS):
                     acc = psum_y.tile([P, N_BANK], F32)
                     for g in range(PASSES):
                         nc.tensor.matmul_mx(
                             out=acc[:],
-                            lhsT=x_codes[:, t, g, :].bitcast(FP8X4),
-                            lhsT_scale=x_scales[:, t, g, :],
+                            lhsT=x_codes[:, g, :].bitcast(FP8X4),
+                            lhsT_scale=x_scales[:, g, :],
                             rhs=w_codes[:, g, 4 * h * N_BANK : 4 * (h + 1) * N_BANK].bitcast(FP8X4),
                             rhs_scale=w_planes[:, g, h * N_BANK : (h + 1) * N_BANK],
                             start=(g == 0),
                             stop=(g == PASSES - 1),
                         )
-                    accs.append(acc)
-            acc_of[blk] = accs
+                    acc_of[(i, h)] = acc
 
         def add_bias_block(blk):
-            accs = acc_of.pop(blk)
             kinds = kinds_pool.tile([P, KINDS, TILES, PER_KIND], F32)
-            for t in range(TILES):
+            for t, i in enumerate(tiles_of(blk)):
                 for h in range(BANKS):
                     cols = slice(h * PER_KIND_BANK, (h + 1) * PER_KIND_BANK)
                     nc.vector.scalar_tensor_tensor(
                         out=kinds[:, :, t, cols],
-                        in0=accs[t * BANKS + h][:].rearrange("p (j a) -> p a j", a=KINDS),
+                        in0=acc_of.pop((i, h))[:].rearrange("p (j a) -> p a j", a=KINDS),
                         scalar=1.0 / TWO_PI,
                         in1=bias_turns[:, :, cols],
                         op0=ALU.mult,
                         op1=ALU.add,
                     )
+            kinds_of[blk] = kinds
+
+        def round_sin_block(blk):
             shifted = kinds_pool.tile([P, TILES, PER_KIND], F32)
-            wrapped = kinds_pool.tile([P, TILES, PER_KIND], F32)
             nc.vector.tensor_scalar(
-                out=shifted[:], in0=kinds[:, 1], scalar1=ROUND_MAGIC, scalar2=None, op0=ALU.add
+                out=shifted[:], in0=kinds_of[blk][:, SIN], scalar1=ROUND_MAGIC, scalar2=None, op0=ALU.add
             )
+            wrap_of[blk] = shifted
+
+        def wrap_sin_block(blk):
+            wrapped = kinds_pool.tile([P, TILES, PER_KIND], F32)
             nc.vector.scalar_tensor_tensor(
                 out=wrapped[:],
-                in0=shifted[:],
+                in0=wrap_of[blk][:],
                 scalar=ROUND_MAGIC,
-                in1=kinds[:, 1],
+                in1=kinds_of[blk][:, SIN],
                 op0=ALU.subtract,
                 op1=ALU.subtract,
             )
-            kinds_of[blk] = (kinds, wrapped)
+            wrap_of[blk] = wrapped
 
-        def activate_block(blk):
-            kinds, wrapped = kinds_of[blk]
-            nc.scalar.activation(out=kinds[:, 3], in_=kinds[:, 3], func=ACT.Tanh, scale=TWO_PI / 2.0)
-            nc.scalar.activation(out=kinds[:, 0], in_=kinds[:, 0], func=ACT.Tanh, scale=TWO_PI)
-            nc.scalar.activation(out=kinds[:, 2], in_=kinds[:, 2], func=ACT.Relu, scale=TWO_PI)
-            nc.scalar.activation(out=kinds[:, 1], in_=wrapped[:], func=ACT.Sin, scale=-TWO_PI)
+        def relu_block(blk):
+            plane = kinds_of[blk][:, RELU]
+            nc.vector.tensor_scalar(out=plane, in0=plane, scalar1=0.0, scalar2=TWO_PI, op0=ALU.max, op1=ALU.mult)
 
-        def finish_block(blk):
-            kinds, wrapped = kinds_of.pop(blk)
-            nc.vector.tensor_scalar(
-                out=kinds[:, 3], in0=kinds[:, 3], scalar1=0.5, scalar2=0.5, op0=ALU.mult, op1=ALU.add
+        def tanh_block(blk):
+            kinds = kinds_of[blk]
+            nc.scalar.activation(out=kinds[:, SIGMOID], in_=kinds[:, SIGMOID], func=ACT.Tanh, scale=TWO_PI / 2.0)
+            nc.scalar.activation(out=kinds[:, TANH], in_=kinds[:, TANH], func=ACT.Tanh, scale=TWO_PI)
+
+        def sin_block(blk):
+            nc.scalar.activation(out=kinds_of[blk][:, SIN], in_=wrap_of.pop(blk)[:], func=ACT.Sin, scale=-TWO_PI)
+
+        def sigmoid_block(blk):
+            plane = kinds_of[blk][:, SIGMOID]
+            nc.vector.tensor_scalar(out=plane, in0=plane, scalar1=0.5, scalar2=0.5, op0=ALU.mult, op1=ALU.add)
+
+        def store_block(blk):
+            kinds = kinds_of.pop(blk)
+            first, second = tiles_of(blk)
+            result_a = out_pool.tile([P, OUT_F], F32)
+            nc.scalar.copy(
+                out=result_a[:].rearrange("p (j a) -> p j a", a=KINDS),
+                in_=kinds[:, :, 0, :].rearrange("p a j -> p j a"),
             )
-            result = out_pool.tile([P, TILES, OUT_F], F32)
-            in_order = result[:].rearrange("p t (j a) -> p (t j) a", a=KINDS)
-            by_kind = kinds[:].rearrange("p a t j -> p (t j) a")
-            cut_1 = SCALAR_GROUPS
-            cut_2 = SCALAR_GROUPS + GPSIMD_GROUPS
-            nc.scalar.copy(out=in_order[:, 0:cut_1, :], in_=by_kind[:, 0:cut_1, :])
+            nc.sync.dma_start(out=out_rows[:, first, :], in_=result_a[:])
+            result_b = out_pool.tile([P, OUT_F], F32)
             nc.gpsimd.tensor_scalar(
-                out=in_order[:, cut_1:cut_2, :],
-                in0=by_kind[:, cut_1:cut_2, :],
+                out=result_b[:].rearrange("p (j a) -> p j a", a=KINDS),
+                in0=kinds[:, :, 1, :].rearrange("p a j -> p j a"),
                 scalar1=1.0,
                 scalar2=0.0,
                 op0=ALU.mult,
                 op1=ALU.add,
             )
-            nc.vector.tensor_copy(out=in_order[:, cut_2:, :], in_=by_kind[:, cut_2:, :])
-            nc.sync.dma_start(out=out_rows[:, blk * TILES : (blk + 1) * TILES, :], in_=result[:])
+            nc.sync.dma_start(out=out_rows[:, second, :], in_=result_b[:])
 
-        for step in range(BLOCKS + 3):
-            if step < BLOCKS:
-                transpose_block(step)
-            if 0 <= step - 1 < BLOCKS:
-                quantise_block(step - 1)
-                multiply_block(step - 1)
-            if 0 <= step - 2 < BLOCKS:
-                add_bias_block(step - 2)
-                activate_block(step - 2)
-            if 0 <= step - 3 < BLOCKS:
-                finish_block(step - 3)
+        def live(blk):
+            return 0 <= blk < BLOCKS
+
+        for s in range(-3, BLOCKS + 1):
+            if live(s - 1):
+                sigmoid_block(s - 1)
+                sin_block(s - 1)
+            if live(s + 1):
+                multiply_block(s + 1)
+            if live(s):
+                add_bias_block(s)
+            if live(s + 2):
+                regroup_block(s + 2)
+            if live(s - 1):
+                store_block(s - 1)
+            if live(s + 3):
+                transpose_block(s + 3)
+            if live(s + 2):
+                quantise_tile((s + 2) * TILES)
+            if live(s):
+                round_sin_block(s)
+                relu_block(s)
+                wrap_sin_block(s)
+            if live(s + 2):
+                quantise_tile((s + 2) * TILES + 1)
+            if live(s):
+                tanh_block(s)

@@ -17,17 +17,28 @@ ROWS, IN_F, OUT_F = 2048, 1024, 1024
 FLOPS = 2 * ROWS * IN_F * OUT_F
 
 P = 128
-K_PASS = 4 * P
+PACK = 4
+K_PASS = PACK * P
 PASSES = IN_F // K_PASS
+X_WORDS = PACK // 2
+WORDS_PASS = K_PASS // 2
+QUADRANT = 32
+LIVE_ROWS = 4
+PSUM_BANKS = 8
 N_BANK = 512
-BANKS = OUT_F // N_BANK
+HALVES = OUT_F // N_BANK
 KINDS = 4
 TANH, SIN, RELU, SIGMOID = 0, 1, 2, 3
 PER_KIND = OUT_F // KINDS
 PER_KIND_BANK = N_BANK // KINDS
 ROW_TILES = ROWS // P
 TILES = 2
-BLOCKS = ROW_TILES // TILES
+BATCHES = ROW_TILES // TILES
+
+TRANSPOSE_AHEAD = 3
+QUANTISE_AHEAD = 2
+MULTIPLY_AHEAD = 1
+FINISH_BEHIND = 1
 
 TWO_PI = 2.0 * math.pi
 ROUND_MAGIC = 1.5 * 2.0**23
@@ -46,31 +57,37 @@ def tile_vdl_kernel(tc, x, w_words, w_scales, b, out):
         kinds_pool = ctx.enter_context(tc.tile_pool(name="kinds", bufs=3))
         out_pool = ctx.enter_context(tc.tile_pool(name="outs", bufs=3))
         psum_t = ctx.enter_context(tc.psum_pool(name="psum_t", bufs=TILES))
-        psum_y = ctx.enter_context(tc.psum_pool(name="psum_y", bufs=6))
+        psum_y = ctx.enter_context(tc.psum_pool(name="psum_y", bufs=PSUM_BANKS - TILES))
         ctx.enter_context(tc.manual_schedule())
 
-        w_planes = consts.tile([P, PASSES, OUT_F], U8, align_bytes=64)
-        nc.vector.memset(w_planes[:].bitcast(I32), 0)
         b_rows = consts.tile([P, OUT_F], BF16)
         nc.vector.memset(b_rows[:], 0.0)
         nc.scalar.dma_start(out=b_rows[0:1, :], in_=b.rearrange("(o n) -> o n", o=1))
-        x_tiles = []
-        for i in range(ROW_TILES):
-            x_tile = x_pool.tile([P, IN_F], BF16)
-            x_tiles.append(x_tile)
-        for i in range(2 * TILES):
-            nc.sync.dma_start(out=x_tiles[i][:], in_=x_rows[:, i, :])
-        scale_rows = w_scales.rearrange("g (Q r) n -> r Q g n", r=4)
-        for r in range(4):
-            nc.sync.dma_start(out=w_planes[r:P:32, :, :].bitcast(I32), in_=scale_rows[r].bitcast(I32))
-        w_codes = consts.tile([P, PASSES, 4 * OUT_F], U8, align_bytes=64)
+        w_planes = consts.tile([P, PASSES, OUT_F], U8, align_bytes=64)
+        nc.vector.memset(w_planes[:].bitcast(I32), 0)
+
+        x_tiles = {}
+
+        def load_x(batch):
+            for t in range(TILES):
+                x_tile = x_pool.tile([P, IN_F], BF16)
+                nc.sync.dma_start(out=x_tile[:], in_=x_rows[:, batch * TILES + t, :])
+                x_tiles[(batch, t)] = x_tile
+
+        early_batches = TRANSPOSE_AHEAD - MULTIPLY_AHEAD
+        for batch in range(early_batches):
+            load_x(batch)
+        scale_rows = w_scales.rearrange("g (Q r) n -> r Q g n", r=LIVE_ROWS)
+        for r in range(LIVE_ROWS):
+            nc.sync.dma_start(out=w_planes[r:P:QUADRANT, :, :].bitcast(I32), in_=scale_rows[r].bitcast(I32))
+        w_codes = consts.tile([P, PASSES, PACK * OUT_F], U8, align_bytes=64)
         for g in range(PASSES):
             nc.sync.dma_start(
                 out=w_codes[:, g, :].bitcast(I32),
                 in_=w_words[g].rearrange("p n t -> p (n t)").bitcast(I32),
             )
-        for i in range(2 * TILES, ROW_TILES):
-            nc.sync.dma_start(out=x_tiles[i][:], in_=x_rows[:, i, :])
+        for batch in range(early_batches, BATCHES):
+            load_x(batch)
 
         warm = consts.tile([P, 1], F32)
         nc.vector.memset(warm[:], 0.0)
@@ -82,7 +99,7 @@ def tile_vdl_kernel(tc, x, w_words, w_scales, b, out):
         ones = consts.tile([P, P], BF16)
         nc.vector.memset(ones[:], 1.0)
         bias_turns = consts.tile([P, KINDS, PER_KIND], F32)
-        for h in range(BANKS):
+        for h in range(HALVES):
             b_all = psum_y.tile([P, N_BANK], F32, name="acc")
             nc.tensor.matmul(
                 out=b_all[:], lhsT=ones[:], rhs=b_rows[:, h * N_BANK : (h + 1) * N_BANK], start=True, stop=True
@@ -100,117 +117,118 @@ def tile_vdl_kernel(tc, x, w_words, w_scales, b, out):
         codes_of = {}
         acc_of = {}
         kinds_of = {}
-        wrap_of = {}
+        shifted_of = {}
+        wrapped_of = {}
 
-        def tiles_of(blk):
-            return range(blk * TILES, (blk + 1) * TILES)
-
-        def transpose_block(blk):
-            for i in tiles_of(blk):
-                words = x_tiles[i][:].bitcast(F32)
-                flipped = psum_t.tile([P, PASSES, 2, P], F32)
+        def transpose_batch(batch):
+            for t in range(TILES):
+                words = x_tiles[(batch, t)][:].bitcast(F32)
+                flipped = psum_t.tile([P, PASSES, X_WORDS, P], F32)
                 for g in range(PASSES):
-                    for u in range(2):
+                    for u in range(X_WORDS):
                         nc.tensor.transpose(
-                            flipped[:, g, u, :], words[:, 256 * g + u : 256 * (g + 1) : 2], ident[:]
+                            flipped[:, g, u, :],
+                            words[:, WORDS_PASS * g + u : WORDS_PASS * (g + 1) : X_WORDS],
+                            ident[:],
                         )
-                flipped_of[i] = flipped
+                flipped_of[(batch, t)] = flipped
 
-        def regroup_block(blk):
-            for i in tiles_of(blk):
+        def regroup_batch(batch):
+            for t in range(TILES):
                 grouped = grouped_pool.tile([P, IN_F], BF16, align_bytes=64)
                 nc.scalar.copy(
-                    out=grouped[:].bitcast(F32).rearrange("p (g m u) -> p g m u", g=PASSES, u=2),
-                    in_=flipped_of.pop(i)[:].rearrange("p g u m -> p g m u"),
+                    out=grouped[:].bitcast(F32).rearrange("p (g m u) -> p g m u", g=PASSES, u=X_WORDS),
+                    in_=flipped_of.pop((batch, t))[:].rearrange("p g u m -> p g m u"),
                 )
-                grouped_of[i] = grouped
+                grouped_of[(batch, t)] = grouped
 
-        def quantise_tile(i):
+        def quantise_tile(batch, t):
             x_codes = codes_pool.tile([P, PASSES, P], U32, align_bytes=64)
             x_scales = codes_pool.tile([P, PASSES, P], U8, align_bytes=64)
             nc.vector.quantize_mx(
                 out=x_codes[:].rearrange("p g m -> p (g m)").bitcast(FP8X4),
                 scales=x_scales[:].rearrange("p g m -> p (g m)"),
-                in_=grouped_of.pop(i)[:],
+                in_=grouped_of.pop((batch, t))[:],
             )
-            codes_of[i] = (x_codes, x_scales)
+            codes_of[(batch, t)] = (x_codes, x_scales)
 
-        def multiply_block(blk):
-            for i in tiles_of(blk):
-                x_codes, x_scales = codes_of.pop(i)
-                for h in range(BANKS):
+        def multiply_batch(batch):
+            for t in range(TILES):
+                x_codes, x_scales = codes_of.pop((batch, t))
+                for h in range(HALVES):
                     acc = psum_y.tile([P, N_BANK], F32)
                     for g in range(PASSES):
                         nc.tensor.matmul_mx(
                             out=acc[:],
                             lhsT=x_codes[:, g, :].bitcast(FP8X4),
                             lhsT_scale=x_scales[:, g, :],
-                            rhs=w_codes[:, g, 4 * h * N_BANK : 4 * (h + 1) * N_BANK].bitcast(FP8X4),
+                            rhs=w_codes[:, g, PACK * h * N_BANK : PACK * (h + 1) * N_BANK].bitcast(FP8X4),
                             rhs_scale=w_planes[:, g, h * N_BANK : (h + 1) * N_BANK],
                             start=(g == 0),
                             stop=(g == PASSES - 1),
                         )
-                    acc_of[(i, h)] = acc
+                    acc_of[(batch, t, h)] = acc
 
-        def add_bias_block(blk):
+        def add_bias_batch(batch):
             kinds = kinds_pool.tile([P, KINDS, TILES, PER_KIND], F32)
-            for t, i in enumerate(tiles_of(blk)):
-                for h in range(BANKS):
+            for t in range(TILES):
+                for h in range(HALVES):
                     cols = slice(h * PER_KIND_BANK, (h + 1) * PER_KIND_BANK)
                     nc.vector.scalar_tensor_tensor(
                         out=kinds[:, :, t, cols],
-                        in0=acc_of.pop((i, h))[:].rearrange("p (j a) -> p a j", a=KINDS),
+                        in0=acc_of.pop((batch, t, h))[:].rearrange("p (j a) -> p a j", a=KINDS),
                         scalar=1.0 / TWO_PI,
                         in1=bias_turns[:, :, cols],
                         op0=ALU.mult,
                         op1=ALU.add,
                     )
-            kinds_of[blk] = kinds
+            kinds_of[batch] = kinds
 
-        def round_sin_block(blk):
+        def shift_sin_batch(batch):
             shifted = kinds_pool.tile([P, TILES, PER_KIND], F32)
             nc.vector.tensor_scalar(
-                out=shifted[:], in0=kinds_of[blk][:, SIN], scalar1=ROUND_MAGIC, scalar2=None, op0=ALU.add
+                out=shifted[:], in0=kinds_of[batch][:, SIN], scalar1=ROUND_MAGIC, scalar2=None, op0=ALU.add
             )
-            wrap_of[blk] = shifted
+            shifted_of[batch] = shifted
 
-        def wrap_sin_block(blk):
+        def wrap_sin_batch(batch):
             wrapped = kinds_pool.tile([P, TILES, PER_KIND], F32)
             nc.vector.scalar_tensor_tensor(
                 out=wrapped[:],
-                in0=wrap_of[blk][:],
+                in0=shifted_of.pop(batch)[:],
                 scalar=ROUND_MAGIC,
-                in1=kinds_of[blk][:, SIN],
+                in1=kinds_of[batch][:, SIN],
                 op0=ALU.subtract,
                 op1=ALU.subtract,
             )
-            wrap_of[blk] = wrapped
+            wrapped_of[batch] = wrapped
 
-        def relu_block(blk):
-            plane = kinds_of[blk][:, RELU]
-            nc.vector.tensor_scalar(out=plane, in0=plane, scalar1=0.0, scalar2=TWO_PI, op0=ALU.max, op1=ALU.mult)
+        def relu_batch(batch):
+            part = kinds_of[batch][:, RELU]
+            nc.vector.tensor_scalar(out=part, in0=part, scalar1=0.0, scalar2=TWO_PI, op0=ALU.max, op1=ALU.mult)
 
-        def tanh_block(blk):
-            kinds = kinds_of[blk]
+        def tanh_batch(batch):
+            kinds = kinds_of[batch]
             nc.scalar.activation(out=kinds[:, SIGMOID], in_=kinds[:, SIGMOID], func=ACT.Tanh, scale=TWO_PI / 2.0)
             nc.scalar.activation(out=kinds[:, TANH], in_=kinds[:, TANH], func=ACT.Tanh, scale=TWO_PI)
 
-        def sin_block(blk):
-            nc.scalar.activation(out=kinds_of[blk][:, SIN], in_=wrap_of.pop(blk)[:], func=ACT.Sin, scale=-TWO_PI)
+        def sin_batch(batch):
+            nc.scalar.activation(
+                out=kinds_of[batch][:, SIN], in_=wrapped_of.pop(batch)[:], func=ACT.Sin, scale=-TWO_PI
+            )
 
-        def sigmoid_block(blk):
-            plane = kinds_of[blk][:, SIGMOID]
-            nc.vector.tensor_scalar(out=plane, in0=plane, scalar1=0.5, scalar2=0.5, op0=ALU.mult, op1=ALU.add)
+        def sigmoid_batch(batch):
+            part = kinds_of[batch][:, SIGMOID]
+            nc.vector.tensor_scalar(out=part, in0=part, scalar1=0.5, scalar2=0.5, op0=ALU.mult, op1=ALU.add)
 
-        def store_block(blk):
-            kinds = kinds_of.pop(blk)
-            first, second = tiles_of(blk)
+        def store_batch(batch):
+            kinds = kinds_of.pop(batch)
             result_a = out_pool.tile([P, OUT_F], F32)
             nc.scalar.copy(
                 out=result_a[:].rearrange("p (j a) -> p j a", a=KINDS),
                 in_=kinds[:, :, 0, :].rearrange("p a j -> p j a"),
             )
-            nc.sync.dma_start(out=out_rows[:, first, :], in_=result_a[:])
+            nc.sync.dma_start(out=out_rows[:, batch * TILES, :], in_=result_a[:])
             result_b = out_pool.tile([P, OUT_F], F32)
             nc.gpsimd.tensor_scalar(
                 out=result_b[:].rearrange("p (j a) -> p j a", a=KINDS),
@@ -220,32 +238,32 @@ def tile_vdl_kernel(tc, x, w_words, w_scales, b, out):
                 op0=ALU.mult,
                 op1=ALU.add,
             )
-            nc.sync.dma_start(out=out_rows[:, second, :], in_=result_b[:])
+            nc.sync.dma_start(out=out_rows[:, batch * TILES + 1, :], in_=result_b[:])
 
-        def live(blk):
-            return 0 <= blk < BLOCKS
+        def live(batch):
+            return 0 <= batch < BATCHES
 
-        for s in range(-3, BLOCKS + 1):
-            if live(s - 1):
-                sigmoid_block(s - 1)
-                sin_block(s - 1)
-            if live(s + 1):
-                multiply_block(s + 1)
-            if live(s):
-                add_bias_block(s)
-            if live(s + 2):
-                regroup_block(s + 2)
-            if live(s - 1):
-                store_block(s - 1)
-            if live(s + 3):
-                transpose_block(s + 3)
-            if live(s + 2):
-                quantise_tile((s + 2) * TILES)
-            if live(s):
-                round_sin_block(s)
-                relu_block(s)
-                wrap_sin_block(s)
-            if live(s + 2):
-                quantise_tile((s + 2) * TILES + 1)
-            if live(s):
-                tanh_block(s)
+        for step in range(-TRANSPOSE_AHEAD, BATCHES + FINISH_BEHIND):
+            if live(step - FINISH_BEHIND):
+                sigmoid_batch(step - FINISH_BEHIND)
+                sin_batch(step - FINISH_BEHIND)
+            if live(step + MULTIPLY_AHEAD):
+                multiply_batch(step + MULTIPLY_AHEAD)
+            if live(step):
+                add_bias_batch(step)
+            if live(step + QUANTISE_AHEAD):
+                regroup_batch(step + QUANTISE_AHEAD)
+            if live(step - FINISH_BEHIND):
+                store_batch(step - FINISH_BEHIND)
+            if live(step + TRANSPOSE_AHEAD):
+                transpose_batch(step + TRANSPOSE_AHEAD)
+            if live(step + QUANTISE_AHEAD):
+                quantise_tile(step + QUANTISE_AHEAD, 0)
+            if live(step):
+                shift_sin_batch(step)
+                relu_batch(step)
+                wrap_sin_batch(step)
+            if live(step + QUANTISE_AHEAD):
+                quantise_tile(step + QUANTISE_AHEAD, 1)
+            if live(step):
+                tanh_batch(step)

@@ -55,7 +55,7 @@ def tile_vdl_kernel(tc, x, w_words, w_scales, b, out):
         grouped_pool = ctx.enter_context(tc.tile_pool(name="grouped", bufs=2 * TILES))
         codes_pool = ctx.enter_context(tc.tile_pool(name="codes", bufs=3 * TILES))
         kinds_pool = ctx.enter_context(tc.tile_pool(name="kinds", bufs=3))
-        out_pool = ctx.enter_context(tc.tile_pool(name="outs", bufs=3))
+        out_pool = ctx.enter_context(tc.tile_pool(name="outs", bufs=4))
         psum_t = ctx.enter_context(tc.psum_pool(name="psum_t", bufs=TILES))
         psum_y = ctx.enter_context(tc.psum_pool(name="psum_y", bufs=PSUM_BANKS - TILES))
         ctx.enter_context(tc.manual_schedule())
@@ -240,6 +240,19 @@ def tile_vdl_kernel(tc, x, w_words, w_scales, b, out):
             )
             nc.sync.dma_start(out=out_rows[:, batch * TILES + 1, :], in_=result_b[:])
 
+        def store_last_batch(batch):
+            kinds = kinds_of.pop(batch)
+            pieces = [(t, h) for t in range(TILES) for h in range(HALVES)]
+            for t, h in pieces:
+                piece = out_pool.tile([P, N_BANK], F32)
+                in_order = piece[:].rearrange("p (j a) -> p j a", a=KINDS)
+                by_kind = kinds[:, :, t, h * PER_KIND_BANK : (h + 1) * PER_KIND_BANK].rearrange("p a j -> p j a")
+                if (t, h) == pieces[-2]:
+                    nc.scalar.copy(out=in_order, in_=by_kind)
+                else:
+                    nc.vector.tensor_copy(out=in_order, in_=by_kind)
+                nc.sync.dma_start(out=out_rows[:, batch * TILES + t, h * N_BANK : (h + 1) * N_BANK], in_=piece[:])
+
         def live(batch):
             return 0 <= batch < BATCHES
 
@@ -254,7 +267,10 @@ def tile_vdl_kernel(tc, x, w_words, w_scales, b, out):
             if live(step + QUANTISE_AHEAD):
                 regroup_batch(step + QUANTISE_AHEAD)
             if live(step - FINISH_BEHIND):
-                store_batch(step - FINISH_BEHIND)
+                if step - FINISH_BEHIND == BATCHES - 1:
+                    store_last_batch(step - FINISH_BEHIND)
+                else:
+                    store_batch(step - FINISH_BEHIND)
             if live(step + TRANSPOSE_AHEAD):
                 transpose_batch(step + TRANSPOSE_AHEAD)
             if live(step + QUANTISE_AHEAD):

@@ -258,7 +258,6 @@ def tile_vdl_kernel(tc, x, w_words, w_scales, b, out):
 
         for step in range(-TRANSPOSE_AHEAD, BATCHES + FINISH_BEHIND):
             if live(step - FINISH_BEHIND):
-                sigmoid_batch(step - FINISH_BEHIND)
                 sin_batch(step - FINISH_BEHIND)
             if live(step + MULTIPLY_AHEAD):
                 multiply_batch(step + MULTIPLY_AHEAD)
@@ -273,13 +272,14 @@ def tile_vdl_kernel(tc, x, w_words, w_scales, b, out):
                     store_batch(step - FINISH_BEHIND)
             if live(step + TRANSPOSE_AHEAD):
                 transpose_batch(step + TRANSPOSE_AHEAD)
+            if live(step):
+                tanh_batch(step)
             if live(step + QUANTISE_AHEAD):
                 quantise_tile(step + QUANTISE_AHEAD, 0)
             if live(step):
                 shift_sin_batch(step)
                 relu_batch(step)
                 wrap_sin_batch(step)
+                sigmoid_batch(step)
             if live(step + QUANTISE_AHEAD):
                 quantise_tile(step + QUANTISE_AHEAD, 1)
-            if live(step):
-                tanh_batch(step)

@@ -60,11 +60,14 @@ def tile_vdl_kernel(tc, x, w_words, w_scales, b, out):
         psum_y = ctx.enter_context(tc.psum_pool(name="psum_y", bufs=PSUM_BANKS - TILES))
         ctx.enter_context(tc.manual_schedule())
 
+        w_planes = consts.tile([P, PASSES, OUT_F], U8, align_bytes=64)
+        nc.vector.memset(w_planes[:].bitcast(I32), 0)
         b_rows = consts.tile([P, OUT_F], BF16)
         nc.vector.memset(b_rows[:], 0.0)
         nc.scalar.dma_start(out=b_rows[0:1, :], in_=b.rearrange("(o n) -> o n", o=1))
-        w_planes = consts.tile([P, PASSES, OUT_F], U8, align_bytes=64)
-        nc.vector.memset(w_planes[:].bitcast(I32), 0)
+        scale_rows = w_scales.rearrange("g (Q r) n -> r Q g n", r=LIVE_ROWS)
+        for r in range(LIVE_ROWS):
+            nc.sync.dma_start(out=w_planes[r:P:QUADRANT, :, :].bitcast(I32), in_=scale_rows[r].bitcast(I32))
 
         x_tiles = {}
 
@@ -77,9 +80,6 @@ def tile_vdl_kernel(tc, x, w_words, w_scales, b, out):
         early_batches = TRANSPOSE_AHEAD - MULTIPLY_AHEAD
         for batch in range(early_batches):
             load_x(batch)
-        scale_rows = w_scales.rearrange("g (Q r) n -> r Q g n", r=LIVE_ROWS)
-        for r in range(LIVE_ROWS):
-            nc.sync.dma_start(out=w_planes[r:P:QUADRANT, :, :].bitcast(I32), in_=scale_rows[r].bitcast(I32))
         w_codes = consts.tile([P, PASSES, PACK * OUT_F], U8, align_bytes=64)
         for g in range(PASSES):
             nc.sync.dma_start(

@@ -65,20 +65,26 @@ def tile_vdl_kernel(tc, x, w_words, w_scales, b, out):
         b_rows = consts.tile([P, OUT_F], BF16)
         nc.vector.memset(b_rows[:], 0.0)
         nc.scalar.dma_start(out=b_rows[0:1, :], in_=b.rearrange("(o n) -> o n", o=1))
-        scale_rows = w_scales.rearrange("g (Q r) n -> r Q g n", r=LIVE_ROWS)
-        for r in range(LIVE_ROWS):
-            nc.sync.dma_start(out=w_planes[r:P:QUADRANT, :, :].bitcast(I32), in_=scale_rows[r].bitcast(I32))
 
         x_tiles = {}
 
+        def load_x_tile(batch, t):
+            x_tile = x_pool.tile([P, IN_F], BF16)
+            nc.sync.dma_start(out=x_tile[:], in_=x_rows[:, batch * TILES + t, :])
+            x_tiles[(batch, t)] = x_tile
+
         def load_x(batch):
             for t in range(TILES):
-                x_tile = x_pool.tile([P, IN_F], BF16)
-                nc.sync.dma_start(out=x_tile[:], in_=x_rows[:, batch * TILES + t, :])
-                x_tiles[(batch, t)] = x_tile
+                load_x_tile(batch, t)
 
+        load_x_tile(0, 0)
+        scale_rows = w_scales.rearrange("g (Q r) n -> r Q g n", r=LIVE_ROWS)
+        for r in range(LIVE_ROWS):
+            nc.sync.dma_start(out=w_planes[r:P:QUADRANT, :, :].bitcast(I32), in_=scale_rows[r].bitcast(I32))
+        for t in range(1, TILES):
+            load_x_tile(0, t)
         early_batches = TRANSPOSE_AHEAD - MULTIPLY_AHEAD
-        for batch in range(early_batches):
+        for batch in range(1, early_batches):
             load_x(batch)
         w_codes = consts.tile([P, PASSES, PACK * OUT_F], U8, align_bytes=64)
         for g in range(PASSES):

@@ -60,11 +60,11 @@ def tile_vdl_kernel(tc, x, w_words, w_scales, b, out):
         psum_y = ctx.enter_context(tc.psum_pool(name="psum_y", bufs=PSUM_BANKS - TILES))
         ctx.enter_context(tc.manual_schedule())
 
-        w_planes = consts.tile([P, PASSES, OUT_F], U8, align_bytes=64)
-        nc.vector.memset(w_planes[:].bitcast(I32), 0)
         b_rows = consts.tile([P, OUT_F], BF16)
         nc.vector.memset(b_rows[:], 0.0)
         nc.scalar.dma_start(out=b_rows[0:1, :], in_=b.rearrange("(o n) -> o n", o=1))
+        w_planes = consts.tile([P, PASSES, OUT_F], U8, align_bytes=64)
+        nc.vector.memset(w_planes[:].bitcast(I32), 0)
 
         x_tiles = {}
 
@@ -87,11 +87,13 @@ def tile_vdl_kernel(tc, x, w_words, w_scales, b, out):
         for batch in range(1, early_batches):
             load_x(batch)
         w_codes = consts.tile([P, PASSES, PACK * OUT_F], U8, align_bytes=64)
-        for g in range(PASSES):
-            nc.sync.dma_start(
-                out=w_codes[:, g, :].bitcast(I32),
-                in_=w_words[g].rearrange("p n t -> p (n t)").bitcast(I32),
-            )
+        for h in range(HALVES):
+            half = slice(PACK * h * N_BANK, PACK * (h + 1) * N_BANK)
+            for g in range(PASSES):
+                nc.sync.dma_start(
+                    out=w_codes[:, g, half].bitcast(I32),
+                    in_=w_words[g].rearrange("p n t -> p (n t)")[:, half].bitcast(I32),
+                )
         for batch in range(early_batches, BATCHES):
             load_x(batch)
 
@@ -158,10 +160,15 @@ def tile_vdl_kernel(tc, x, w_words, w_scales, b, out):
             )
             codes_of[(batch, t)] = (x_codes, x_scales)
 
+        def banks_of(batch):
+            if batch == 0:
+                return [(t, h) for h in range(HALVES) for t in range(TILES)]
+            return [(t, h) for t in range(TILES) for h in range(HALVES)]
+
         def multiply_batch(batch):
-            for t in range(TILES):
-                x_codes, x_scales = codes_of.pop((batch, t))
-                for h in range(HALVES):
+            for t, h in banks_of(batch):
+                x_codes, x_scales = codes_of[(batch, t)]
+                if True:
                     acc = psum_y.tile([P, N_BANK], F32)
                     for g in range(PASSES):
                         nc.tensor.matmul_mx(
@@ -177,8 +184,8 @@ def tile_vdl_kernel(tc, x, w_words, w_scales, b, out):
 
         def add_bias_batch(batch):
             kinds = kinds_pool.tile([P, KINDS, TILES, PER_KIND], F32)
-            for t in range(TILES):
-                for h in range(HALVES):
+            for t, h in banks_of(batch):
+                if True:
                     cols = slice(h * PER_KIND_BANK, (h + 1) * PER_KIND_BANK)
                     nc.vector.scalar_tensor_tensor(
                         out=kinds[:, :, t, cols],

@@ -25,6 +25,7 @@ WORDS_PASS = K_PASS // 2
 QUADRANT = 32
 LIVE_ROWS = 4
 PSUM_BANKS = 8
+T_BANKS = 3
 N_BANK = 512
 HALVES = OUT_F // N_BANK
 KINDS = 4
@@ -56,8 +57,8 @@ def tile_vdl_kernel(tc, x, w_words, w_scales, b, out):
         codes_pool = ctx.enter_context(tc.tile_pool(name="codes", bufs=3 * TILES))
         kinds_pool = ctx.enter_context(tc.tile_pool(name="kinds", bufs=3))
         out_pool = ctx.enter_context(tc.tile_pool(name="outs", bufs=4))
-        psum_t = ctx.enter_context(tc.psum_pool(name="psum_t", bufs=TILES))
-        psum_y = ctx.enter_context(tc.psum_pool(name="psum_y", bufs=PSUM_BANKS - TILES))
+        psum_t = ctx.enter_context(tc.psum_pool(name="psum_t", bufs=T_BANKS))
+        psum_y = ctx.enter_context(tc.psum_pool(name="psum_y", bufs=PSUM_BANKS - T_BANKS))
         ctx.enter_context(tc.manual_schedule())
 
         b_rows = consts.tile([P, OUT_F], BF16)

@@ -35,6 +35,7 @@ PER_KIND_BANK = N_BANK // KINDS
 ROW_TILES = ROWS // P
 TILES = 2
 BATCHES = ROW_TILES // TILES
+BOTH = slice(0, TILES)
 
 TRANSPOSE_AHEAD = 3
 QUANTISE_AHEAD = 2
@@ -198,42 +199,84 @@ def tile_vdl_kernel(tc, x, w_words, w_scales, b, out):
                     )
             kinds_of[batch] = kinds
 
-        def shift_sin_batch(batch):
-            shifted = kinds_pool.tile([P, TILES, PER_KIND], F32)
+        def shift_sin(batch, tiles=BOTH):
+            if batch not in shifted_of:
+                shifted = kinds_pool.tile([P, TILES, PER_KIND], F32)
+                shifted_of[batch] = shifted
             nc.vector.tensor_scalar(
-                out=shifted[:], in0=kinds_of[batch][:, SIN], scalar1=ROUND_MAGIC, scalar2=None, op0=ALU.add
+                out=shifted_of[batch][:, tiles],
+                in0=kinds_of[batch][:, SIN, tiles],
+                scalar1=ROUND_MAGIC,
+                scalar2=None,
+                op0=ALU.add,
             )
-            shifted_of[batch] = shifted
 
-        def wrap_sin_batch(batch):
-            wrapped = kinds_pool.tile([P, TILES, PER_KIND], F32)
+        def wrap_sin(batch, tiles=BOTH):
+            if batch not in wrapped_of:
+                wrapped = kinds_pool.tile([P, TILES, PER_KIND], F32)
+                wrapped_of[batch] = wrapped
             nc.vector.scalar_tensor_tensor(
-                out=wrapped[:],
-                in0=shifted_of.pop(batch)[:],
+                out=wrapped_of[batch][:, tiles],
+                in0=shifted_of[batch][:, tiles],
                 scalar=ROUND_MAGIC,
-                in1=kinds_of[batch][:, SIN],
+                in1=kinds_of[batch][:, SIN, tiles],
                 op0=ALU.subtract,
                 op1=ALU.subtract,
             )
-            wrapped_of[batch] = wrapped
 
-        def relu_batch(batch):
-            part = kinds_of[batch][:, RELU]
-            nc.vector.tensor_scalar(out=part, in0=part, scalar1=0.0, scalar2=TWO_PI, op0=ALU.max, op1=ALU.mult)
-
-        def tanh_batch(batch):
-            kinds = kinds_of[batch]
-            nc.scalar.activation(out=kinds[:, SIGMOID], in_=kinds[:, SIGMOID], func=ACT.Tanh, scale=TWO_PI / 2.0)
-            nc.scalar.activation(out=kinds[:, TANH], in_=kinds[:, TANH], func=ACT.Tanh, scale=TWO_PI)
-
-        def sin_batch(batch):
+        def sin(batch, tiles=BOTH):
             nc.scalar.activation(
-                out=kinds_of[batch][:, SIN], in_=wrapped_of.pop(batch)[:], func=ACT.Sin, scale=-TWO_PI
+                out=kinds_of[batch][:, SIN, tiles], in_=wrapped_of[batch][:, tiles], func=ACT.Sin, scale=-TWO_PI
             )
 
-        def sigmoid_batch(batch):
-            part = kinds_of[batch][:, SIGMOID]
-            nc.vector.tensor_scalar(out=part, in0=part, scalar1=0.5, scalar2=0.5, op0=ALU.mult, op1=ALU.add)
+        def relu(batch, tiles=BOTH, on_scalar=False):
+            part = kinds_of[batch][:, RELU, tiles]
+            if on_scalar:
+                nc.scalar.activation(out=part, in_=part, func=ACT.Relu, scale=TWO_PI)
+            else:
+                nc.vector.tensor_scalar(out=part, in0=part, scalar1=0.0, scalar2=TWO_PI, op0=ALU.max, op1=ALU.mult)
+
+        def tanh(batch, tiles=BOTH):
+            part = kinds_of[batch][:, TANH, tiles]
+            nc.scalar.activation(out=part, in_=part, func=ACT.Tanh, scale=TWO_PI)
+
+        def half_tanh(batch, tiles=BOTH):
+            part = kinds_of[batch][:, SIGMOID, tiles]
+            nc.scalar.activation(out=part, in_=part, func=ACT.Tanh, scale=TWO_PI / 2.0)
+
+        def sigmoid(batch, tiles=BOTH, on_scalar=False):
+            part = kinds_of[batch][:, SIGMOID, tiles]
+            if on_scalar:
+                nc.scalar.activation(out=part, in_=part, func=ACT.Copy, scale=0.5, bias=0.5)
+            else:
+                nc.vector.tensor_scalar(out=part, in0=part, scalar1=0.5, scalar2=0.5, op0=ALU.mult, op1=ALU.add)
+
+        def finish_last_batch(batch):
+            first, second = slice(0, 1), slice(1, 2)
+            shift_sin(batch, first)
+            wrap_sin(batch, first)
+            shift_sin(batch, second)
+            relu(batch, first)
+            tanh(batch, first)
+            half_tanh(batch, first)
+            half_tanh(batch, second)
+            wrap_sin(batch, second)
+            sigmoid(batch, first, on_scalar=True)
+            sin(batch, first)
+            tanh(batch, second)
+            sigmoid(batch, second)
+            sin(batch, second)
+            relu(batch, second, on_scalar=True)
+            for t in range(TILES):
+                for h in range(HALVES):
+                    piece = out_pool.tile([P, N_BANK], F32)
+                    by_kind = kinds_of[batch][:, :, t, h * PER_KIND_BANK : (h + 1) * PER_KIND_BANK]
+                    nc.vector.tensor_copy(
+                        out=piece[:].rearrange("p (j a) -> p j a", a=KINDS), in_=by_kind.rearrange("p a j -> p j a")
+                    )
+                    nc.sync.dma_start(
+                        out=out_rows[:, batch * TILES + t, h * N_BANK : (h + 1) * N_BANK], in_=piece[:]
+                    )
 
         def store_batch(batch):
             kinds = kinds_of.pop(batch)
@@ -254,25 +297,12 @@ def tile_vdl_kernel(tc, x, w_words, w_scales, b, out):
             )
             nc.sync.dma_start(out=out_rows[:, batch * TILES + 1, :], in_=result_b[:])
 
-        def store_last_batch(batch):
-            kinds = kinds_of.pop(batch)
-            pieces = [(t, h) for t in range(TILES) for h in range(HALVES)]
-            for t, h in pieces:
-                piece = out_pool.tile([P, N_BANK], F32)
-                in_order = piece[:].rearrange("p (j a) -> p j a", a=KINDS)
-                by_kind = kinds[:, :, t, h * PER_KIND_BANK : (h + 1) * PER_KIND_BANK].rearrange("p a j -> p j a")
-                if (t, h) == pieces[-2]:
-                    nc.scalar.copy(out=in_order, in_=by_kind)
-                else:
-                    nc.vector.tensor_copy(out=in_order, in_=by_kind)
-                nc.sync.dma_start(out=out_rows[:, batch * TILES + t, h * N_BANK : (h + 1) * N_BANK], in_=piece[:])
-
         def live(batch):
             return 0 <= batch < BATCHES
 
-        for step in range(-TRANSPOSE_AHEAD, BATCHES + FINISH_BEHIND):
+        for step in range(-TRANSPOSE_AHEAD, BATCHES):
             if live(step - FINISH_BEHIND):
-                sin_batch(step - FINISH_BEHIND)
+                sin(step - FINISH_BEHIND)
             if live(step + MULTIPLY_AHEAD):
                 multiply_batch(step + MULTIPLY_AHEAD)
             if live(step):
@@ -280,20 +310,20 @@ def tile_vdl_kernel(tc, x, w_words, w_scales, b, out):
             if live(step + QUANTISE_AHEAD):
                 regroup_batch(step + QUANTISE_AHEAD)
             if live(step - FINISH_BEHIND):
-                if step - FINISH_BEHIND == BATCHES - 1:
-                    store_last_batch(step - FINISH_BEHIND)
-                else:
-                    store_batch(step - FINISH_BEHIND)
+                store_batch(step - FINISH_BEHIND)
             if live(step + TRANSPOSE_AHEAD):
                 transpose_batch(step + TRANSPOSE_AHEAD)
-            if live(step):
-                tanh_batch(step)
+            if step == BATCHES - 1:
+                finish_last_batch(step)
+            elif live(step):
+                half_tanh(step)
+                tanh(step)
             if live(step + QUANTISE_AHEAD):
                 quantise_tile(step + QUANTISE_AHEAD, 0)
-            if live(step):
-                shift_sin_batch(step)
-                relu_batch(step)
-                wrap_sin_batch(step)
-                sigmoid_batch(step)
+            if live(step) and step < BATCHES - 1:
+                shift_sin(step)
+                relu(step)
+                wrap_sin(step)
+                sigmoid(step)
             if live(step + QUANTISE_AHEAD):
                 quantise_tile(step + QUANTISE_AHEAD, 1)

@@ -65,7 +65,7 @@ def tile_vdl_kernel(tc, x, w_words, w_scales, b, out):
         b_rows = consts.tile([P, OUT_F], BF16)
         nc.vector.memset(b_rows[:], 0.0)
         nc.scalar.dma_start(out=b_rows[0:1, :], in_=b.rearrange("(o n) -> o n", o=1))
-        w_planes = consts.tile([P, PASSES, OUT_F], U8, align_bytes=64)
+        w_planes = consts.tile([P, OUT_F], U8, align_bytes=64)
         nc.vector.memset(w_planes[:].bitcast(I32), 0)
 
         x_tiles = {}
@@ -80,9 +80,13 @@ def tile_vdl_kernel(tc, x, w_words, w_scales, b, out):
                 load_x_tile(batch, t)
 
         load_x_tile(0, 0)
-        scale_rows = w_scales.rearrange("g (Q r) n -> r Q g n", r=LIVE_ROWS)
-        for r in range(LIVE_ROWS):
-            nc.sync.dma_start(out=w_planes[r:P:QUADRANT, :, :].bitcast(I32), in_=scale_rows[r].bitcast(I32))
+        scale_rows = w_scales.rearrange("g (Q r) n -> Q g r n", r=LIVE_ROWS)
+        for quadrant in range(P // QUADRANT):
+            first = QUADRANT * quadrant
+            nc.sync.dma_start(
+                out=w_planes[first : first + PASSES * LIVE_ROWS, :].bitcast(I32),
+                in_=scale_rows[quadrant].bitcast(I32),
+            )
         for t in range(1, TILES):
             load_x_tile(0, t)
         early_batches = TRANSPOSE_AHEAD - MULTIPLY_AHEAD
@@ -178,7 +182,7 @@ def tile_vdl_kernel(tc, x, w_words, w_scales, b, out):
                             lhsT=x_codes[:, g, :].bitcast(FP8X4),
                             lhsT_scale=x_scales[:, g, :],
                             rhs=w_codes[:, g, PACK * h * N_BANK : PACK * (h + 1) * N_BANK].bitcast(FP8X4),
-                            rhs_scale=w_planes[:, g, h * N_BANK : (h + 1) * N_BANK],
+                            rhs_scale=w_planes[LIVE_ROWS * g :, h * N_BANK : (h + 1) * N_BANK],
                             start=(g == 0),
                             stop=(g == PASSES - 1),
                         )

@@ -2,7 +2,6 @@ import math
 from contextlib import ExitStack
 
 import concourse.mybir as mybir
-from concourse.masks import make_identity
 
 F32 = mybir.dt.float32
 BF16 = mybir.dt.bfloat16
@@ -107,8 +106,21 @@ def tile_vdl_kernel(tc, x, w_words, w_scales, b, out):
         nc.vector.memset(warm[:], 0.0)
         nc.scalar.activation(out=warm[:], in_=warm[:], func=ACT.Silu)
 
+        ones_f32 = consts.tile([P, QUADRANT], F32)
+        nc.vector.memset(ones_f32[:], 1.0)
         ident = consts.tile([P, P], F32)
-        make_identity(nc, ident[:])
+        nc.vector.memset(ident[:], 0.0)
+        column = consts.tile([P, QUADRANT], F32, align_bytes=64)
+        nc.vector.tensor_tensor_scan(
+            out=column[:], data0=ones_f32[:], data1=ones_f32[:], initial=0.0, op0=ALU.add, op1=ALU.mult
+        )
+        row = consts.tile([P, QUADRANT], F32, align_bytes=64)
+        nc.vector.transpose(row[:], column[:])
+        for start in range(0, P, QUADRANT):
+            block = slice(start, start + QUADRANT)
+            nc.vector.tensor_tensor(
+                out=ident[block, block], in0=column[block, :], in1=row[block, :], op=ALU.is_equal
+            )
 
         ones = consts.tile([P, P], BF16)
         nc.vector.memset(ones[:], 1.0)

import math
from contextlib import ExitStack

import concourse.mybir as mybir

F32 = mybir.dt.float32
BF16 = mybir.dt.bfloat16
I32 = mybir.dt.int32
U8 = mybir.dt.uint8
U32 = mybir.dt.uint32
FP8X4 = mybir.dt.float8_e4m3fn_x4
ACT = mybir.ActivationFunctionType
ALU = mybir.AluOpType

ROWS, IN_F, OUT_F = 2048, 1024, 1024
FLOPS = 2 * ROWS * IN_F * OUT_F

P = 128
PACK = 4
K_PASS = PACK * P
PASSES = IN_F // K_PASS
X_WORDS = PACK // 2
WORDS_PASS = K_PASS // 2
QUADRANT = 32
LIVE_ROWS = 4
PSUM_BANKS = 8
T_BANKS = 3
N_BANK = 512
HALVES = OUT_F // N_BANK
KINDS = 4
TANH, SIN, RELU, SIGMOID = 0, 1, 2, 3
PER_KIND = OUT_F // KINDS
PER_KIND_BANK = N_BANK // KINDS
ROW_TILES = ROWS // P
TILES = 2
BATCHES = ROW_TILES // TILES
BOTH = slice(0, TILES)

TRANSPOSE_AHEAD = 3
QUANTISE_AHEAD = 2
MULTIPLY_AHEAD = 1
FINISH_BEHIND = 1

TWO_PI = 2.0 * math.pi
ROUND_MAGIC = 1.5 * 2.0**23


def tile_vdl_kernel(tc, x, w_words, w_scales, b, out):
    nc = tc.nc
    x_rows = x.rearrange("(p i) k -> p i k", i=ROW_TILES)
    out_rows = out.rearrange("(p i) n -> p i n", i=ROW_TILES)

    with ExitStack() as ctx:
        consts = ctx.enter_context(tc.tile_pool(name="consts", bufs=1))
        x_pool = ctx.enter_context(tc.tile_pool(name="x", bufs=ROW_TILES))
        grouped_pool = ctx.enter_context(tc.tile_pool(name="grouped", bufs=2 * TILES))
        codes_pool = ctx.enter_context(tc.tile_pool(name="codes", bufs=3 * TILES))
        kinds_pool = ctx.enter_context(tc.tile_pool(name="kinds", bufs=3))
        out_pool = ctx.enter_context(tc.tile_pool(name="outs", bufs=4))
        psum_t = ctx.enter_context(tc.psum_pool(name="psum_t", bufs=T_BANKS))
        psum_y = ctx.enter_context(tc.psum_pool(name="psum_y", bufs=PSUM_BANKS - T_BANKS))
        ctx.enter_context(tc.manual_schedule())

        b_rows = consts.tile([P, OUT_F], BF16)
        nc.vector.memset(b_rows[:], 0.0)
        nc.scalar.dma_start(out=b_rows[0:1, :], in_=b.rearrange("(o n) -> o n", o=1))
        w_planes = consts.tile([P, OUT_F], U8, align_bytes=64)
        nc.vector.memset(w_planes[:].bitcast(I32), 0)

        x_tiles = {}

        def load_x_tile(batch, t):
            x_tile = x_pool.tile([P, IN_F], BF16)
            nc.sync.dma_start(out=x_tile[:], in_=x_rows[:, batch * TILES + t, :])
            x_tiles[(batch, t)] = x_tile

        def load_x(batch):
            for t in range(TILES):
                load_x_tile(batch, t)

        load_x_tile(0, 0)
        scale_rows = w_scales.rearrange("g (Q r) n -> Q g r n", r=LIVE_ROWS)
        for quadrant in range(P // QUADRANT):
            first = QUADRANT * quadrant
            nc.sync.dma_start(
                out=w_planes[first : first + PASSES * LIVE_ROWS, :].bitcast(I32),
                in_=scale_rows[quadrant].bitcast(I32),
            )
        for t in range(1, TILES):
            load_x_tile(0, t)
        early_batches = TRANSPOSE_AHEAD - MULTIPLY_AHEAD
        for batch in range(1, early_batches):
            load_x(batch)
        w_codes = consts.tile([P, PASSES, PACK * OUT_F], U8, align_bytes=64)
        for h in range(HALVES):
            half = slice(PACK * h * N_BANK, PACK * (h + 1) * N_BANK)
            for g in range(PASSES):
                nc.sync.dma_start(
                    out=w_codes[:, g, half].bitcast(I32),
                    in_=w_words[g].rearrange("p n t -> p (n t)")[:, half].bitcast(I32),
                )
        for batch in range(early_batches, BATCHES):
            load_x(batch)

        warm = consts.tile([P, 1], F32)
        nc.vector.memset(warm[:], 0.0)
        nc.scalar.activation(out=warm[:], in_=warm[:], func=ACT.Silu)

        ones_f32 = consts.tile([P, QUADRANT], F32)
        nc.vector.memset(ones_f32[:], 1.0)
        ident = consts.tile([P, P], F32)
        nc.vector.memset(ident[:], 0.0)
        column = consts.tile([P, QUADRANT], F32, align_bytes=64)
        nc.vector.tensor_tensor_scan(
            out=column[:], data0=ones_f32[:], data1=ones_f32[:], initial=0.0, op0=ALU.add, op1=ALU.mult
        )
        row = consts.tile([P, QUADRANT], F32, align_bytes=64)
        nc.vector.transpose(row[:], column[:])
        for start in range(0, P, QUADRANT):
            block = slice(start, start + QUADRANT)
            nc.vector.tensor_tensor(
                out=ident[block, block], in0=column[block, :], in1=row[block, :], op=ALU.is_equal
            )

        ones = consts.tile([P, P], BF16)
        nc.vector.memset(ones[:], 1.0)
        bias_turns = consts.tile([P, KINDS, PER_KIND], F32)
        for h in range(HALVES):
            b_all = psum_y.tile([P, N_BANK], F32, name="acc")
            nc.tensor.matmul(
                out=b_all[:], lhsT=ones[:], rhs=b_rows[:, h * N_BANK : (h + 1) * N_BANK], start=True, stop=True
            )
            nc.vector.tensor_scalar(
                out=bias_turns[:, :, h * PER_KIND_BANK : (h + 1) * PER_KIND_BANK],
                in0=b_all[:].rearrange("p (j a) -> p a j", a=KINDS),
                scalar1=1.0 / TWO_PI,
                scalar2=None,
                op0=ALU.mult,
            )

        flipped_of = {}
        grouped_of = {}
        codes_of = {}
        acc_of = {}
        kinds_of = {}
        shifted_of = {}
        wrapped_of = {}

        def transpose_batch(batch):
            for t in range(TILES):
                words = x_tiles[(batch, t)][:].bitcast(F32)
                flipped = psum_t.tile([P, PASSES, X_WORDS, P], F32)
                for g in range(PASSES):
                    for u in range(X_WORDS):
                        nc.tensor.transpose(
                            flipped[:, g, u, :],
                            words[:, WORDS_PASS * g + u : WORDS_PASS * (g + 1) : X_WORDS],
                            ident[:],
                        )
                flipped_of[(batch, t)] = flipped

        def regroup_batch(batch):
            for t in range(TILES):
                grouped = grouped_pool.tile([P, IN_F], BF16, align_bytes=64)
                nc.scalar.copy(
                    out=grouped[:].bitcast(F32).rearrange("p (g m u) -> p g m u", g=PASSES, u=X_WORDS),
                    in_=flipped_of.pop((batch, t))[:].rearrange("p g u m -> p g m u"),
                )
                grouped_of[(batch, t)] = grouped

        def quantise_tile(batch, t):
            x_codes = codes_pool.tile([P, PASSES, P], U32, align_bytes=64)
            x_scales = codes_pool.tile([P, PASSES, P], U8, align_bytes=64)
            nc.vector.quantize_mx(
                out=x_codes[:].rearrange("p g m -> p (g m)").bitcast(FP8X4),
                scales=x_scales[:].rearrange("p g m -> p (g m)"),
                in_=grouped_of.pop((batch, t))[:],
            )
            codes_of[(batch, t)] = (x_codes, x_scales)

        def banks_of(batch):
            if batch == 0:
                return [(t, h) for h in range(HALVES) for t in range(TILES)]
            return [(t, h) for t in range(TILES) for h in range(HALVES)]

        def multiply_batch(batch):
            for t, h in banks_of(batch):
                x_codes, x_scales = codes_of[(batch, t)]
                if True:
                    acc = psum_y.tile([P, N_BANK], F32)
                    for g in range(PASSES):
                        nc.tensor.matmul_mx(
                            out=acc[:],
                            lhsT=x_codes[:, g, :].bitcast(FP8X4),
                            lhsT_scale=x_scales[:, g, :],
                            rhs=w_codes[:, g, PACK * h * N_BANK : PACK * (h + 1) * N_BANK].bitcast(FP8X4),
                            rhs_scale=w_planes[LIVE_ROWS * g :, h * N_BANK : (h + 1) * N_BANK],
                            start=(g == 0),
                            stop=(g == PASSES - 1),
                        )
                    acc_of[(batch, t, h)] = acc

        def add_bias_batch(batch):
            kinds = kinds_pool.tile([P, KINDS, TILES, PER_KIND], F32)
            for t, h in banks_of(batch):
                if True:
                    cols = slice(h * PER_KIND_BANK, (h + 1) * PER_KIND_BANK)
                    nc.vector.scalar_tensor_tensor(
                        out=kinds[:, :, t, cols],
                        in0=acc_of.pop((batch, t, h))[:].rearrange("p (j a) -> p a j", a=KINDS),
                        scalar=1.0 / TWO_PI,
                        in1=bias_turns[:, :, cols],
                        op0=ALU.mult,
                        op1=ALU.add,
                    )
            kinds_of[batch] = kinds

        def shift_sin(batch, tiles=BOTH):
            if batch not in shifted_of:
                shifted = kinds_pool.tile([P, TILES, PER_KIND], F32)
                shifted_of[batch] = shifted
            nc.vector.tensor_scalar(
                out=shifted_of[batch][:, tiles],
                in0=kinds_of[batch][:, SIN, tiles],
                scalar1=ROUND_MAGIC,
                scalar2=None,
                op0=ALU.add,
            )

        def wrap_sin(batch, tiles=BOTH):
            if batch not in wrapped_of:
                wrapped = kinds_pool.tile([P, TILES, PER_KIND], F32)
                wrapped_of[batch] = wrapped
            nc.vector.scalar_tensor_tensor(
                out=wrapped_of[batch][:, tiles],
                in0=shifted_of[batch][:, tiles],
                scalar=ROUND_MAGIC,
                in1=kinds_of[batch][:, SIN, tiles],
                op0=ALU.subtract,
                op1=ALU.subtract,
            )

        def sin(batch, tiles=BOTH):
            nc.scalar.activation(
                out=kinds_of[batch][:, SIN, tiles], in_=wrapped_of[batch][:, tiles], func=ACT.Sin, scale=-TWO_PI
            )

        def relu(batch, tiles=BOTH, on_scalar=False):
            part = kinds_of[batch][:, RELU, tiles]
            if on_scalar:
                nc.scalar.activation(out=part, in_=part, func=ACT.Relu, scale=TWO_PI)
            else:
                nc.vector.tensor_scalar(out=part, in0=part, scalar1=0.0, scalar2=TWO_PI, op0=ALU.max, op1=ALU.mult)

        def tanh(batch, tiles=BOTH):
            part = kinds_of[batch][:, TANH, tiles]
            nc.scalar.activation(out=part, in_=part, func=ACT.Tanh, scale=TWO_PI)

        def half_tanh(batch, tiles=BOTH):
            part = kinds_of[batch][:, SIGMOID, tiles]
            nc.scalar.activation(out=part, in_=part, func=ACT.Tanh, scale=TWO_PI / 2.0)

        def sigmoid(batch, tiles=BOTH, on_scalar=False):
            part = kinds_of[batch][:, SIGMOID, tiles]
            if on_scalar:
                nc.scalar.activation(out=part, in_=part, func=ACT.Copy, scale=0.5, bias=0.5)
            else:
                nc.vector.tensor_scalar(out=part, in0=part, scalar1=0.5, scalar2=0.5, op0=ALU.mult, op1=ALU.add)

        def finish_last_batch(batch):
            first, second = slice(0, 1), slice(1, 2)
            shift_sin(batch, first)
            wrap_sin(batch, first)
            shift_sin(batch, second)
            relu(batch, first)
            tanh(batch, first)
            half_tanh(batch, first)
            half_tanh(batch, second)
            wrap_sin(batch, second)
            sigmoid(batch, first, on_scalar=True)
            sin(batch, first)
            tanh(batch, second)
            sigmoid(batch, second)
            sin(batch, second)
            relu(batch, second, on_scalar=True)
            for t in range(TILES):
                for h in range(HALVES):
                    piece = out_pool.tile([P, N_BANK], F32)
                    by_kind = kinds_of[batch][:, :, t, h * PER_KIND_BANK : (h + 1) * PER_KIND_BANK]
                    nc.vector.tensor_copy(
                        out=piece[:].rearrange("p (j a) -> p j a", a=KINDS), in_=by_kind.rearrange("p a j -> p j a")
                    )
                    nc.sync.dma_start(
                        out=out_rows[:, batch * TILES + t, h * N_BANK : (h + 1) * N_BANK], in_=piece[:]
                    )

        def store_batch(batch):
            kinds = kinds_of.pop(batch)
            result_a = out_pool.tile([P, OUT_F], F32)
            nc.scalar.copy(
                out=result_a[:].rearrange("p (j a) -> p j a", a=KINDS),
                in_=kinds[:, :, 0, :].rearrange("p a j -> p j a"),
            )
            nc.sync.dma_start(out=out_rows[:, batch * TILES, :], in_=result_a[:])
            result_b = out_pool.tile([P, OUT_F], F32)
            nc.gpsimd.tensor_scalar(
                out=result_b[:].rearrange("p (j a) -> p j a", a=KINDS),
                in0=kinds[:, :, 1, :].rearrange("p a j -> p j a"),
                scalar1=1.0,
                scalar2=0.0,
                op0=ALU.mult,
                op1=ALU.add,
            )
            nc.sync.dma_start(out=out_rows[:, batch * TILES + 1, :], in_=result_b[:])

        def live(batch):
            return 0 <= batch < BATCHES

        for step in range(-TRANSPOSE_AHEAD, BATCHES):
            if live(step - FINISH_BEHIND):
                sin(step - FINISH_BEHIND)
            if live(step + MULTIPLY_AHEAD):
                multiply_batch(step + MULTIPLY_AHEAD)
            if live(step):
                add_bias_batch(step)
            if live(step + QUANTISE_AHEAD):
                regroup_batch(step + QUANTISE_AHEAD)
            if live(step - FINISH_BEHIND):
                store_batch(step - FINISH_BEHIND)
            if live(step + TRANSPOSE_AHEAD):
                transpose_batch(step + TRANSPOSE_AHEAD)
            if step == BATCHES - 1:
                finish_last_batch(step)
            elif live(step):
                half_tanh(step)
                tanh(step)
            if live(step + QUANTISE_AHEAD):
                quantise_tile(step + QUANTISE_AHEAD, 0)
            if live(step) and step < BATCHES - 1:
                shift_sin(step)
                relu(step)
                wrap_sin(step)
                sigmoid(step)
            if live(step + QUANTISE_AHEAD):
                quantise_tile(step + QUANTISE_AHEAD, 1)
